import numpy as np
import ml_dtypes


def mxq(x, axis, fmt="e4m3"):
    dtype, down = {"e4m3": (ml_dtypes.float8_e4m3fn, 7), "e5m2": (ml_dtypes.float8_e5m2, 14)}[fmt]
    v = np.moveaxis(np.asarray(x, np.float32).astype(ml_dtypes.bfloat16).astype(np.float64), axis, -1)
    blocks = v.reshape(v.shape[:-1] + (-1, 32))
    amax = np.abs(blocks).max(-1, keepdims=True)
    byte = np.maximum(np.where(amax > 0, np.frexp(amax)[1] - 1 + 127, 0) - down, 1)
    scale = np.exp2(byte - 127.0)
    codes = (blocks / scale).astype(np.float32).astype(dtype).astype(np.float64)
    return np.moveaxis((codes * scale).reshape(v.shape), -1, axis)


WIDE = False


def mx_kscale(k):
    if not WIDE:
        return np.ones(k)
    levels = np.array([10, -10, 5, -5, 0])
    a = np.random.permutation(np.resize(levels, k // 512 * 4)).reshape(k // 512, 4)
    idx = np.arange(k)
    return np.exp2(a[idx // 512, idx % 128 // 32])


BF16 = ml_dtypes.bfloat16


def bf(x):
    return np.asarray(x, np.float32).astype(BF16)


def f64(x):
    return np.asarray(x).astype(np.float64)


N_A, N_P, D = 512, 8192, 512
TEMPERATURE = 0.07
SIG = 3.5
SA = np.sqrt(SIG * TEMPERATURE / np.sqrt(D))
SP = SA * np.sqrt(SIG ** 2 - 2.0 * np.log(N_P / N_A)) / SIG


def logsumexp(v):
    m = v.max(axis=1, keepdims=True)
    return m[:, 0] + np.log(np.exp(v - m).sum(axis=1))


def setup_inputs():
    s = mx_kscale(D)
    c = np.mean(s ** 4) ** -0.25
    return {"anchor": bf(np.random.standard_normal((N_A, D)) * SA * s * c),
            "pos": bf(np.random.standard_normal((N_P, D)) * SP / (s * c))}


def reference(anchor, pos):
    aq = mxq(f64(anchor), 1, "e4m3")
    sim_pos = (aq @ mxq(f64(pos), 1, "e4m3").T) / TEMPERATURE
    sim_neg = (aq @ aq.T) / TEMPERATURE
    sim_neg = np.where(np.eye(aq.shape[0], dtype=bool), -np.inf, sim_neg)
    numerator = logsumexp(sim_pos)
    denominator = np.logaddexp(numerator, logsumexp(sim_neg))
    return numerator - denominator

@@ -1,0 +1,203 @@
+from contextlib import ExitStack
+
+import concourse.mybir as mybir
+from concourse.masks import make_identity
+
+F32 = mybir.dt.float32
+BF16 = mybir.dt.bfloat16
+U32 = mybir.dt.uint32
+U8 = mybir.dt.uint8
+FP8X4 = mybir.dt.float8_e4m3fn_x4
+ALU = mybir.AluOpType
+ACT = mybir.ActivationFunctionType
+AXIS = mybir.AxisListType
+
+P = 128
+N_A, N_P, D = 512, 8192, 512
+TEMPERATURE = 0.07
+FLOPS = 2 * N_A * D * (N_P + N_A)
+
+PACK = 4
+WORDS = D // 2
+A_TILES = N_A // P
+PASS_COLS = 512
+LOAD_ROWS = 512
+PASSES = 2
+LAST = PASSES - 1
+BLOCK = PASSES * PASS_COLS
+N_BLOCKS = N_P // BLOCK
+BLOCK_ROW_TILES = BLOCK // P
+AHEAD = 3
+N_STATS = N_BLOCKS + 1
+NEGATIVES = N_BLOCKS
+BANK_ROW_TILES = 2
+VECTOR_EVERY = 4
+MASKED = 1.0e38
+
+
+def transpose_rows(nc, psum_words, identity, raw_words, grouped_words):
+    for bank in range(raw_words.shape[1] // BANK_ROW_TILES):
+        flipped = psum_words.tile([P, 2, BANK_ROW_TILES * P], F32, name="flipped")
+        for half in range(2):
+            for i in range(BANK_ROW_TILES):
+                nc.tensor.transpose(
+                    flipped[:, half, i * P : (i + 1) * P],
+                    raw_words[:, bank * BANK_ROW_TILES + i, half * P : (half + 1) * P],
+                    identity[:],
+                )
+        rows = slice(bank * BANK_ROW_TILES * P, (bank + 1) * BANK_ROW_TILES * P)
+        if bank % VECTOR_EVERY == VECTOR_EVERY - 1:
+            nc.vector.tensor_copy(out=grouped_words[:, rows, :], in_=flipped[:].rearrange("p u c -> p c u"))
+        else:
+            nc.scalar.copy(out=grouped_words[:, rows, :], in_=flipped[:].rearrange("p u c -> p c u"))
+
+
+def tile_crossgenderinfonceloss_pa_t_kernel(tc, anchor, pos, out):
+    nc = tc.nc
+    with ExitStack() as ctx:
+        keep = ctx.enter_context(tc.tile_pool(name="keep", bufs=1))
+        stage = ctx.enter_context(tc.tile_pool(name="stage", bufs=3))
+        psum_words = ctx.enter_context(tc.psum_pool(name="psum_words", bufs=4))
+        psum_scores = ctx.enter_context(tc.psum_pool(name="psum_scores", bufs=4))
+        ctx.enter_context(tc.manual_schedule())
+
+        a_raw = keep.tile([P, A_TILES * D], BF16)
+        nc.sync.dma_start(
+            out=a_raw[:].rearrange("p (t k) -> p t k", t=A_TILES),
+            in_=anchor.rearrange("(t p) k -> p t k", p=P),
+        )
+        p_raw = keep.tile([P, (N_P // P) * D], BF16)
+        load_cols = (LOAD_ROWS // P) * D
+        pos_loads = pos.rearrange("(c p r) k -> c p (r k)", p=P, r=LOAD_ROWS // P)
+        for c in range(N_P // LOAD_ROWS):
+            nc.sync.dma_start(out=p_raw[:, c * load_cols : (c + 1) * load_cols], in_=pos_loads[c])
+        a_raw_words = a_raw[:].bitcast(F32).rearrange("p (r w) -> p r w", w=WORDS)
+        p_raw_words = p_raw[:].bitcast(F32).rearrange("p (r w) -> p r w", w=WORDS)
+
+        identity = keep.tile([P, P], F32)
+        make_identity(nc, identity[:])
+        result = keep.tile([P, P], F32)
+        nc.vector.memset(result[:], 0.0)
+
+        a_codes = keep.tile([P, N_A], U32, align_bytes=64)
+        a_scales = keep.tile([P, N_A], U8, align_bytes=64)
+        p_codes = keep.tile([P, N_P], U32, align_bytes=64)
+        p_scales = keep.tile([P, N_P], U8, align_bytes=64)
+        lowest = keep.tile([P, A_TILES, N_STATS, PASSES], F32)
+        sums = keep.tile([P, A_TILES, N_STATS], F32)
+
+        def transpose_block(b):
+            grouped = stage.tile([P, BLOCK * PACK], BF16, name="grouped", bufs=AHEAD, align_bytes=64)
+            transpose_rows(
+                nc, psum_words, identity,
+                p_raw_words[:, b * BLOCK_ROW_TILES : (b + 1) * BLOCK_ROW_TILES, :],
+                grouped[:].bitcast(F32).rearrange("p (c u) -> p c u", u=2),
+            )
+            return grouped
+
+        def quantise_block(b, grouped):
+            nc.vector.quantize_mx(
+                out=p_codes[:, b * BLOCK : (b + 1) * BLOCK].bitcast(FP8X4),
+                scales=p_scales[:, b * BLOCK : (b + 1) * BLOCK],
+                in_=grouped[:],
+            )
+
+        def scores(t, moving_codes, moving_scales):
+            acc = psum_scores.tile([P, PASS_COLS], F32, name="acc")
+            nc.tensor.matmul_mx(
+                out=acc[:],
+                lhsT=a_codes[:, t * P : (t + 1) * P].bitcast(FP8X4),
+                lhsT_scale=a_scales[:, t * P : (t + 1) * P],
+                rhs=moving_codes.bitcast(FP8X4),
+                rhs_scale=moving_scales,
+                start=True,
+                stop=True,
+            )
+            return acc
+
+        def score_block(b):
+            x = [stage.tile([P, BLOCK], F32, name="x%d" % t) for t in range(A_TILES)]
+            for first in range(0, A_TILES, 2):
+                for h in range(PASSES):
+                    cols = slice(b * BLOCK + h * PASS_COLS, b * BLOCK + (h + 1) * PASS_COLS)
+                    for t in (first, first + 1):
+                        acc = scores(t, p_codes[:, cols], p_scales[:, cols])
+                        nc.vector.tensor_scalar(
+                            out=x[t][:, h * PASS_COLS : (h + 1) * PASS_COLS], in0=acc[:],
+                            scalar1=-1.0 / TEMPERATURE,
+                            scalar2=None if h == 0 else lowest[:, t, b, h - 1 : h],
+                            op0=ALU.mult, op1=ALU.min,
+                            accum_out=lowest[:, t, b, h : h + 1],
+                        )
+            return x
+
+        def score_negatives():
+            x = [stage.tile([P, N_A], F32, name="x_neg%d" % t, bufs=1) for t in range(A_TILES)]
+            for t in range(A_TILES):
+                acc = scores(t, a_codes[:], a_scales[:])
+                nc.scalar.mul(out=x[t][:], in_=acc[:], mul=-1.0 / TEMPERATURE)
+                own = x[t][:, t * P : (t + 1) * P]
+                nc.gpsimd.affine_select(
+                    out=own, in_=own, pattern=[[-1, P]], compare_op=ALU.not_equal,
+                    fill=MASKED, base=0, channel_multiplier=1,
+                )
+                nc.vector.tensor_reduce(
+                    out=lowest[:, t, NEGATIVES, LAST : LAST + 1], in_=x[t][:], axis=AXIS.X, op=ALU.min
+                )
+            return x
+
+        def exponentials(s, x):
+            for t in range(A_TILES):
+                nc.scalar.activation(
+                    out=x[t][:], in_=x[t][:], func=ACT.Exp,
+                    bias=lowest[:, t, s, LAST : LAST + 1], scale=-1.0,
+                    accum_out=sums[:, t, s : s + 1],
+                )
+
+        a_grouped = keep.tile([P, N_A * PACK], BF16, align_bytes=64)
+        transpose_rows(
+            nc, psum_words, identity, a_raw_words,
+            a_grouped[:].bitcast(F32).rearrange("p (c u) -> p c u", u=2),
+        )
+        nc.vector.quantize_mx(out=a_codes[:].bitcast(FP8X4), scales=a_scales[:], in_=a_grouped[:])
+        grouped = {0: transpose_block(0)}
+        quantise_block(0, grouped[0])
+        x_negatives = score_negatives()
+        for b in range(1, AHEAD):
+            grouped[b] = transpose_block(b)
+        exponentials(NEGATIVES, x_negatives)
+
+        for b in range(N_BLOCKS):
+            if b + 1 < N_BLOCKS:
+                quantise_block(b + 1, grouped[b + 1])
+            x = score_block(b)
+            if b + AHEAD < N_BLOCKS:
+                grouped[b + AHEAD] = transpose_block(b + AHEAD)
+            exponentials(b, x)
+
+        ALL, POSITIVES = 0, 1
+        low = keep.tile([P, A_TILES, 2], F32)
+        nc.vector.tensor_reduce(out=low[:, :, ALL], in_=lowest[:, :, :, LAST], axis=AXIS.X, op=ALU.min)
+        nc.vector.tensor_reduce(
+            out=low[:, :, POSITIVES], in_=lowest[:, :, 0:N_BLOCKS, LAST], axis=AXIS.X, op=ALU.min
+        )
+        both = [P, A_TILES, 2, N_STATS]
+        weight = keep.tile(both, F32)
+        nc.vector.tensor_tensor(
+            out=weight[:], in0=low[:].unsqueeze(3).to_broadcast(both),
+            in1=lowest[:, :, :, LAST].unsqueeze(2).to_broadcast(both), op=ALU.subtract,
+        )
+        nc.vector.memset(weight[:, :, POSITIVES, NEGATIVES], -MASKED)
+        nc.scalar.activation(out=weight[:], in_=weight[:], func=ACT.Exp)
+        nc.vector.tensor_mul(out=weight[:], in0=weight[:], in1=sums[:].unsqueeze(2).to_broadcast(both))
+        lse = keep.tile([P, A_TILES, 2], F32)
+        nc.vector.tensor_reduce(out=lse[:], in_=weight[:], axis=AXIS.X, op=ALU.add)
+        nc.scalar.activation(out=lse[:], in_=lse[:], func=ACT.Ln)
+        nc.vector.tensor_sub(out=lse[:], in0=lse[:], in1=low[:])
+        nc.vector.tensor_sub(out=result[:, 0:A_TILES], in0=lse[:, :, POSITIVES], in1=lse[:, :, ALL])
+
+        result_rows_psum = psum_words.tile([P, P], F32, name="flipped")
+        nc.tensor.transpose(result_rows_psum[:], result[:], identity[:])
+        result_rows = keep.tile([P, P], F32)
+        nc.vector.tensor_copy(out=result_rows[:], in_=result_rows_psum[:])
+        nc.sync.dma_start(out=out.rearrange("(t p) -> t p", p=P), in_=result_rows[0:A_TILES, :])

@@ -27,7 +27,7 @@ LAST = PASSES - 1
 BLOCK = PASSES * PASS_COLS
 N_BLOCKS = N_P // BLOCK
 BLOCK_ROW_TILES = BLOCK // P
-AHEAD = 3
+AHEAD = 2
 N_STATS = N_BLOCKS + 1
 NEGATIVES = N_BLOCKS
 BANK_ROW_TILES = 2
@@ -115,21 +115,18 @@ def tile_crossgenderinfonceloss_pa_t_kernel(tc, anchor, pos, out):
             )
             return acc
 
-        def score_block(b):
-            x = [stage.tile([P, BLOCK], F32, name="x%d" % t) for t in range(A_TILES)]
-            for first in range(0, A_TILES, 2):
-                for h in range(PASSES):
-                    cols = slice(b * BLOCK + h * PASS_COLS, b * BLOCK + (h + 1) * PASS_COLS)
-                    for t in (first, first + 1):
-                        acc = scores(t, p_codes[:, cols], p_scales[:, cols])
-                        nc.vector.tensor_scalar(
-                            out=x[t][:, h * PASS_COLS : (h + 1) * PASS_COLS], in0=acc[:],
-                            scalar1=-1.0 / TEMPERATURE,
-                            scalar2=None if h == 0 else lowest[:, t, b, h - 1 : h],
-                            op0=ALU.mult, op1=ALU.min,
-                            accum_out=lowest[:, t, b, h : h + 1],
-                        )
-            return x
+        def score_pair(b, x, first):
+            for h in range(PASSES):
+                cols = slice(b * BLOCK + h * PASS_COLS, b * BLOCK + (h + 1) * PASS_COLS)
+                for t in (first, first + 1):
+                    acc = scores(t, p_codes[:, cols], p_scales[:, cols])
+                    nc.vector.tensor_scalar(
+                        out=x[t][:, h * PASS_COLS : (h + 1) * PASS_COLS], in0=acc[:],
+                        scalar1=-1.0 / TEMPERATURE,
+                        scalar2=None if h == 0 else lowest[:, t, b, h - 1 : h],
+                        op0=ALU.mult, op1=ALU.min,
+                        accum_out=lowest[:, t, b, h : h + 1],
+                    )
 
         def score_negatives():
             x = [stage.tile([P, N_A], F32, name="x_neg%d" % t, bufs=1) for t in range(A_TILES)]
@@ -170,9 +167,11 @@ def tile_crossgenderinfonceloss_pa_t_kernel(tc, anchor, pos, out):
         for b in range(N_BLOCKS):
             if b + 1 < N_BLOCKS:
                 quantise_block(b + 1, grouped[b + 1])
-            x = score_block(b)
+            x = [stage.tile([P, BLOCK], F32, name="x%d" % t) for t in range(A_TILES)]
+            score_pair(b, x, 0)
             if b + AHEAD < N_BLOCKS:
                 grouped[b + AHEAD] = transpose_block(b + AHEAD)
+            score_pair(b, x, 2)
             exponentials(b, x)
 
         ALL, POSITIVES = 0, 1

@@ -59,7 +59,6 @@ def tile_crossgenderinfonceloss_pa_t_kernel(tc, anchor, pos, out):
         stage = ctx.enter_context(tc.tile_pool(name="stage", bufs=3))
         psum_words = ctx.enter_context(tc.psum_pool(name="psum_words", bufs=4))
         psum_scores = ctx.enter_context(tc.psum_pool(name="psum_scores", bufs=4))
-        ctx.enter_context(tc.manual_schedule())
 
         a_raw = keep.tile([P, A_TILES * D], BF16)
         nc.sync.dma_start(

from contextlib import ExitStack

import concourse.mybir as mybir
from concourse.masks import make_identity

F32 = mybir.dt.float32
BF16 = mybir.dt.bfloat16
U32 = mybir.dt.uint32
U8 = mybir.dt.uint8
FP8X4 = mybir.dt.float8_e4m3fn_x4
ALU = mybir.AluOpType
ACT = mybir.ActivationFunctionType
AXIS = mybir.AxisListType

P = 128
N_A, N_P, D = 512, 8192, 512
TEMPERATURE = 0.07
FLOPS = 2 * N_A * D * (N_P + N_A)

PACK = 4
WORDS = D // 2
A_TILES = N_A // P
PASS_COLS = 512
LOAD_ROWS = 512
PASSES = 2
LAST = PASSES - 1
BLOCK = PASSES * PASS_COLS
N_BLOCKS = N_P // BLOCK
BLOCK_ROW_TILES = BLOCK // P
AHEAD = 2
N_STATS = N_BLOCKS + 1
NEGATIVES = N_BLOCKS
BANK_ROW_TILES = 2
VECTOR_EVERY = 4
MASKED = 1.0e38


def transpose_rows(nc, psum_words, identity, raw_words, grouped_words):
    for bank in range(raw_words.shape[1] // BANK_ROW_TILES):
        flipped = psum_words.tile([P, 2, BANK_ROW_TILES * P], F32, name="flipped")
        for half in range(2):
            for i in range(BANK_ROW_TILES):
                nc.tensor.transpose(
                    flipped[:, half, i * P : (i + 1) * P],
                    raw_words[:, bank * BANK_ROW_TILES + i, half * P : (half + 1) * P],
                    identity[:],
                )
        rows = slice(bank * BANK_ROW_TILES * P, (bank + 1) * BANK_ROW_TILES * P)
        if bank % VECTOR_EVERY == VECTOR_EVERY - 1:
            nc.vector.tensor_copy(out=grouped_words[:, rows, :], in_=flipped[:].rearrange("p u c -> p c u"))
        else:
            nc.scalar.copy(out=grouped_words[:, rows, :], in_=flipped[:].rearrange("p u c -> p c u"))


def tile_crossgenderinfonceloss_pa_t_kernel(tc, anchor, pos, out):
    nc = tc.nc
    with ExitStack() as ctx:
        keep = ctx.enter_context(tc.tile_pool(name="keep", bufs=1))
        stage = ctx.enter_context(tc.tile_pool(name="stage", bufs=3))
        psum_words = ctx.enter_context(tc.psum_pool(name="psum_words", bufs=4))
        psum_scores = ctx.enter_context(tc.psum_pool(name="psum_scores", bufs=4))

        a_raw = keep.tile([P, A_TILES * D], BF16)
        nc.sync.dma_start(
            out=a_raw[:].rearrange("p (t k) -> p t k", t=A_TILES),
            in_=anchor.rearrange("(t p) k -> p t k", p=P),
        )
        p_raw = keep.tile([P, (N_P // P) * D], BF16)
        load_cols = (LOAD_ROWS // P) * D
        pos_loads = pos.rearrange("(c p r) k -> c p (r k)", p=P, r=LOAD_ROWS // P)
        for c in range(N_P // LOAD_ROWS):
            nc.sync.dma_start(out=p_raw[:, c * load_cols : (c + 1) * load_cols], in_=pos_loads[c])
        a_raw_words = a_raw[:].bitcast(F32).rearrange("p (r w) -> p r w", w=WORDS)
        p_raw_words = p_raw[:].bitcast(F32).rearrange("p (r w) -> p r w", w=WORDS)

        identity = keep.tile([P, P], F32)
        make_identity(nc, identity[:])
        result = keep.tile([P, P], F32)
        nc.vector.memset(result[:], 0.0)

        a_codes = keep.tile([P, N_A], U32, align_bytes=64)
        a_scales = keep.tile([P, N_A], U8, align_bytes=64)
        p_codes = keep.tile([P, N_P], U32, align_bytes=64)
        p_scales = keep.tile([P, N_P], U8, align_bytes=64)
        lowest = keep.tile([P, A_TILES, N_STATS, PASSES], F32)
        sums = keep.tile([P, A_TILES, N_STATS], F32)

        def transpose_block(b):
            grouped = stage.tile([P, BLOCK * PACK], BF16, name="grouped", bufs=AHEAD, align_bytes=64)
            transpose_rows(
                nc, psum_words, identity,
                p_raw_words[:, b * BLOCK_ROW_TILES : (b + 1) * BLOCK_ROW_TILES, :],
                grouped[:].bitcast(F32).rearrange("p (c u) -> p c u", u=2),
            )
            return grouped

        def quantise_block(b, grouped):
            nc.vector.quantize_mx(
                out=p_codes[:, b * BLOCK : (b + 1) * BLOCK].bitcast(FP8X4),
                scales=p_scales[:, b * BLOCK : (b + 1) * BLOCK],
                in_=grouped[:],
            )

        def scores(t, moving_codes, moving_scales):
            acc = psum_scores.tile([P, PASS_COLS], F32, name="acc")
            nc.tensor.matmul_mx(
                out=acc[:],
                lhsT=a_codes[:, t * P : (t + 1) * P].bitcast(FP8X4),
                lhsT_scale=a_scales[:, t * P : (t + 1) * P],
                rhs=moving_codes.bitcast(FP8X4),
                rhs_scale=moving_scales,
                start=True,
                stop=True,
            )
            return acc

        def score_pair(b, x, first):
            for h in range(PASSES):
                cols = slice(b * BLOCK + h * PASS_COLS, b * BLOCK + (h + 1) * PASS_COLS)
                for t in (first, first + 1):
                    acc = scores(t, p_codes[:, cols], p_scales[:, cols])
                    nc.vector.tensor_scalar(
                        out=x[t][:, h * PASS_COLS : (h + 1) * PASS_COLS], in0=acc[:],
                        scalar1=-1.0 / TEMPERATURE,
                        scalar2=None if h == 0 else lowest[:, t, b, h - 1 : h],
                        op0=ALU.mult, op1=ALU.min,
                        accum_out=lowest[:, t, b, h : h + 1],
                    )

        def score_negatives():
            x = [stage.tile([P, N_A], F32, name="x_neg%d" % t, bufs=1) for t in range(A_TILES)]
            for t in range(A_TILES):
                acc = scores(t, a_codes[:], a_scales[:])
                nc.scalar.mul(out=x[t][:], in_=acc[:], mul=-1.0 / TEMPERATURE)
                own = x[t][:, t * P : (t + 1) * P]
                nc.gpsimd.affine_select(
                    out=own, in_=own, pattern=[[-1, P]], compare_op=ALU.not_equal,
                    fill=MASKED, base=0, channel_multiplier=1,
                )
                nc.vector.tensor_reduce(
                    out=lowest[:, t, NEGATIVES, LAST : LAST + 1], in_=x[t][:], axis=AXIS.X, op=ALU.min
                )
            return x

        def exponentials(s, x):
            for t in range(A_TILES):
                nc.scalar.activation(
                    out=x[t][:], in_=x[t][:], func=ACT.Exp,
                    bias=lowest[:, t, s, LAST : LAST + 1], scale=-1.0,
                    accum_out=sums[:, t, s : s + 1],
                )

        a_grouped = keep.tile([P, N_A * PACK], BF16, align_bytes=64)
        transpose_rows(
            nc, psum_words, identity, a_raw_words,
            a_grouped[:].bitcast(F32).rearrange("p (c u) -> p c u", u=2),
        )
        nc.vector.quantize_mx(out=a_codes[:].bitcast(FP8X4), scales=a_scales[:], in_=a_grouped[:])
        grouped = {0: transpose_block(0)}
        quantise_block(0, grouped[0])
        x_negatives = score_negatives()
        for b in range(1, AHEAD):
            grouped[b] = transpose_block(b)
        exponentials(NEGATIVES, x_negatives)

        for b in range(N_BLOCKS):
            if b + 1 < N_BLOCKS:
                quantise_block(b + 1, grouped[b + 1])
            x = [stage.tile([P, BLOCK], F32, name="x%d" % t) for t in range(A_TILES)]
            score_pair(b, x, 0)
            if b + AHEAD < N_BLOCKS:
                grouped[b + AHEAD] = transpose_block(b + AHEAD)
            score_pair(b, x, 2)
            exponentials(b, x)

        ALL, POSITIVES = 0, 1
        low = keep.tile([P, A_TILES, 2], F32)
        nc.vector.tensor_reduce(out=low[:, :, ALL], in_=lowest[:, :, :, LAST], axis=AXIS.X, op=ALU.min)
        nc.vector.tensor_reduce(
            out=low[:, :, POSITIVES], in_=lowest[:, :, 0:N_BLOCKS, LAST], axis=AXIS.X, op=ALU.min
        )
        both = [P, A_TILES, 2, N_STATS]
        weight = keep.tile(both, F32)
        nc.vector.tensor_tensor(
            out=weight[:], in0=low[:].unsqueeze(3).to_broadcast(both),
            in1=lowest[:, :, :, LAST].unsqueeze(2).to_broadcast(both), op=ALU.subtract,
        )
        nc.vector.memset(weight[:, :, POSITIVES, NEGATIVES], -MASKED)
        nc.scalar.activation(out=weight[:], in_=weight[:], func=ACT.Exp)
        nc.vector.tensor_mul(out=weight[:], in0=weight[:], in1=sums[:].unsqueeze(2).to_broadcast(both))
        lse = keep.tile([P, A_TILES, 2], F32)
        nc.vector.tensor_reduce(out=lse[:], in_=weight[:], axis=AXIS.X, op=ALU.add)
        nc.scalar.activation(out=lse[:], in_=lse[:], func=ACT.Ln)
        nc.vector.tensor_sub(out=lse[:], in0=lse[:], in1=low[:])
        nc.vector.tensor_sub(out=result[:, 0:A_TILES], in0=lse[:, :, POSITIVES], in1=lse[:, :, ALL])

        result_rows_psum = psum_words.tile([P, P], F32, name="flipped")
        nc.tensor.transpose(result_rows_psum[:], result[:], identity[:])
        result_rows = keep.tile([P, P], F32)
        nc.vector.tensor_copy(out=result_rows[:], in_=result_rows_psum[:])
        nc.sync.dma_start(out=out.rearrange("(t p) -> t p", p=P), in_=result_rows[0:A_TILES, :])
